import numpy as np
import ml_dtypes


def mxq(x, axis, fmt="e4m3"):
    dtype, down = {"e4m3": (ml_dtypes.float8_e4m3fn, 7), "e5m2": (ml_dtypes.float8_e5m2, 14)}[fmt]
    v = np.moveaxis(np.asarray(x, np.float32).astype(ml_dtypes.bfloat16).astype(np.float64), axis, -1)
    blocks = v.reshape(v.shape[:-1] + (-1, 32))
    amax = np.abs(blocks).max(-1, keepdims=True)
    byte = np.maximum(np.where(amax > 0, np.frexp(amax)[1] - 1 + 127, 0) - down, 1)
    scale = np.exp2(byte - 127.0)
    codes = (blocks / scale).astype(np.float32).astype(dtype).astype(np.float64)
    return np.moveaxis((codes * scale).reshape(v.shape), -1, axis)


WIDE = False


def mx_kscale(k):
    if not WIDE:
        return np.ones(k)
    levels = np.array([10, -10, 5, -5, 0])
    if k % 512:
        return np.exp2(np.random.permutation(np.resize(levels, k // 32))).repeat(32)
    a = np.empty((k // 512, 16))
    for p in range(k // 512):
        a[p, :8] = np.random.permutation(np.resize(levels, 8))
        for g in range(8):
            far = levels[np.abs(levels - a[p, g]) >= 10]
            a[p, g + 8] = far[np.random.randint(len(far))]
    return np.exp2(a.ravel()).repeat(32)


BF16 = ml_dtypes.bfloat16


def bf(x):
    return np.asarray(x, np.float32).astype(BF16)


def f64(x):
    return np.asarray(x).astype(np.float64)


E2M1 = np.array([0.0, 0.5, 1.0, 1.5, 2.0, 3.0, 4.0, 6.0, -0.0, -0.5, -1.0, -1.5, -2.0, -3.0, -4.0, -6.0])


def pack_weight(w, fmt):
    k, n = w.shape
    w = f64(bf(w)).reshape(k // 32, 32, n)
    amax = np.abs(w).max(1)
    if fmt == "e4m3":
        byte = np.frexp(amax)[1] - 1 + 127 - 7
    else:
        mant, ex = np.frexp(amax / 6.0)
        byte = np.where(mant > 0.5, ex, ex - 1) + 127
    byte = np.clip(np.where(amax > 0, byte, 1), 1, 254)
    scaled = (w * np.exp2(127.0 - byte)[:, None, :]).reshape(k, n).astype(np.float32)
    by_word = np.ascontiguousarray(scaled.reshape(k // 512, 128, 4, n).transpose(0, 1, 3, 2))
    if fmt == "e4m3":
        words = by_word.astype(ml_dtypes.float8_e4m3fn).view(np.uint8)
    else:
        c = by_word.astype(ml_dtypes.float4_e2m1fn).view(np.uint8) & 0xF
        words = c[..., 0::2] | (c[..., 1::2] << 4)
    return np.ascontiguousarray(words), np.ascontiguousarray(byte.astype(np.uint8).reshape(k // 512, 16, n))


def unpack_weight(words, scales, fmt):
    g, p, n, _ = words.shape
    if fmt == "e4m3":
        vals = np.ascontiguousarray(words).view(ml_dtypes.float8_e4m3fn).astype(np.float64)
    else:
        nib = np.empty((g, p, n, 4), np.uint8)
        nib[..., 0::2] = words & 0xF
        nib[..., 1::2] = words >> 4
        vals = E2M1[nib]
    vals = vals * np.repeat(np.exp2(scales.astype(np.float64) - 127.0), 8, axis=1)[..., None]
    return vals.transpose(0, 1, 3, 2).reshape(g * 512, n)


B, T, C, H, D, L = 1, 512, 2048, 16, 128, 512
THETA = 1.0e4


def rope(u, cos, sin):
    u0, u1 = u[..., 0::2], u[..., 1::2]
    c = cos[None, :, None, :]
    s = sin[None, :, None, :]
    o0 = u0 * c - u1 * s
    o1 = u0 * s + u1 * c
    return np.stack([o0, o1], axis=-1).reshape(u.shape)


def draw0():
    s, t = mx_kscale(C), mx_kscale(L)
    inv_freq = 1.0 / (THETA ** (np.arange(0, D, 2) / D))
    ang = np.outer(np.arange(T), inv_freq)
    x = bf(np.random.standard_normal((B, T, C)) * s)
    wq_words, wq_scales = pack_weight((np.random.standard_normal((H * D, C)) * 2.0 / np.sqrt(C) / s).T, "e4m3")
    wkv_down_words, wkv_down_scales = pack_weight((np.random.standard_normal((L, C)) / np.sqrt(C) / s * t[:, None]).T, "e4m3")
    wk_up_words, wk_up_scales = pack_weight((np.random.standard_normal((D, L)) / np.sqrt(L) / t).T, "e4m3")
    wv_up_words, wv_up_scales = pack_weight((np.random.standard_normal((D, L)) / np.sqrt(L) / t).T, "e4m3")
    return {"x": x,
            "freqs_cos": bf(np.cos(ang)),
            "freqs_sin": bf(np.sin(ang)),
            "wq_words": wq_words,
            "wq_scales": wq_scales,
            "wkv_down_words": wkv_down_words,
            "wkv_down_scales": wkv_down_scales,
            "wk_up_words": wk_up_words,
            "wk_up_scales": wk_up_scales,
            "wv_up_words": wv_up_words,
            "wv_up_scales": wv_up_scales}


def core(x, freqs_cos, freqs_sin, wq_words, wq_scales, wkv_down_words, wkv_down_scales, wk_up_words, wk_up_scales, wv_up_words, wv_up_scales):
    cos, sin = f64(freqs_cos), f64(freqs_sin)
    xq = mxq(f64(x), 2, "e4m3")
    q = (xq @ unpack_weight(wq_words, wq_scales, "e4m3")).reshape(B, T, H, D)
    kv_latent = xq @ unpack_weight(wkv_down_words, wkv_down_scales, "e4m3")
    lq = mxq(kv_latent, 2, "e4m3")
    k = lq @ unpack_weight(wk_up_words, wk_up_scales, "e4m3")
    v = lq @ unpack_weight(wv_up_words, wv_up_scales, "e4m3")
    q_rot = rope(q, cos, sin)
    k_rot = rope(k[:, :, None, :], cos, sin)[:, :, 0, :]
    return q_rot, k_rot, v


def e4m3fn_bytes(y):
    return np.clip(np.asarray(y, np.float64), -448.0, 448.0).astype(np.float32).astype(ml_dtypes.float8_e4m3fn).view(np.uint8)


def e4m3fn_values(b):
    return np.asarray(b, np.uint8).view(ml_dtypes.float8_e4m3fn).astype(np.float64)


def setup_inputs():
    d = draw0()
    x0 = np.asarray(d['x']).astype(np.float64)
    s = (np.max(np.abs(x0), axis=(0, 1), keepdims=True) / 448.0).astype(np.float32)
    out = {}
    for k, v in d.items():
        if k == 'x':
            out['x_bytes'] = e4m3fn_bytes(x0 / s.astype(np.float64))
            out['x_scale'] = s
        else:
            out[k] = v
    return out


def reference(x_bytes, x_scale, freqs_cos, freqs_sin, wq_words, wq_scales, wkv_down_words, wkv_down_scales, wk_up_words, wk_up_scales, wv_up_words, wv_up_scales):
    return core(e4m3fn_values(x_bytes) * x_scale.astype(np.float64), freqs_cos, freqs_sin, wq_words, wq_scales, wkv_down_words, wkv_down_scales, wk_up_words, wk_up_scales, wv_up_words, wv_up_scales)

@@ -1,0 +1,291 @@
+from contextlib import ExitStack
+
+import concourse.mybir as mybir
+from concourse.masks import make_identity
+
+T, C, HEADS, D, L = 512, 2048, 16, 128, 512
+FLOPS = 2 * T * C * (HEADS * D + L) + 2 * T * L * 2 * D
+
+F32 = mybir.dt.float32
+BF16 = mybir.dt.bfloat16
+I32 = mybir.dt.int32
+U32 = mybir.dt.uint32
+U8 = mybir.dt.uint8
+FP8 = mybir.dt.float8_e4m3fn
+FP8X4 = mybir.dt.float8_e4m3fn_x4
+MULT = mybir.AluOpType.mult
+ADD = mybir.AluOpType.add
+
+P = 128
+G = C // 512
+MT = T // P
+HALF = 256
+NQ = (HEADS * D) // 512
+
+
+def tile_attention_pa_w8_kernel(
+    tc, x_bytes, x_scale, freqs_cos, freqs_sin,
+    wq_words, wq_scales, wd_words, wd_scales, wk_words, wk_scales, wv_words, wv_scales,
+    q_out, k_out, v_out,
+):
+    nc = tc.nc
+    with ExitStack() as ctx:
+        keep = ctx.enter_context(tc.tile_pool(name="keep", bufs=1))
+        work = ctx.enter_context(tc.tile_pool(name="work", bufs=3))
+        outs = ctx.enter_context(tc.tile_pool(name="outs", bufs=4))
+        psum = ctx.enter_context(tc.psum_pool(name="psum", bufs=1))
+        ctx.enter_context(tc.manual_schedule())
+
+        def bank(i, shape, label):
+            t = psum.tile(shape, F32, name="bank%d" % (i % 8), tag="bank%d" % (i % 8))
+            return t
+
+        ident = keep.tile([P, P], F32)
+        make_identity(nc, ident[:])
+        wd_sc = keep.tile([P, L], U8, align_bytes=64)
+        wq_sc = keep.tile([P, HEADS * D], U8, align_bytes=64)
+        wu_sc = keep.tile([P, 2 * D], U8, align_bytes=64)
+        nc.vector.memset(wd_sc[:].bitcast(I32), 0)
+        nc.vector.memset(wq_sc[:].bitcast(I32), 0)
+        nc.vector.memset(wu_sc[:].bitcast(I32), 0)
+
+        x_rows = x_bytes.rearrange("b (m p) k -> p (b m) k", p=P)
+        xsc = keep.tile([P, G, 4], F32)
+        nc.scalar.dma_start(out=xsc[:], in_=x_scale.rearrange("a b (g p t) -> p (a b g) t", p=P, t=4))
+        x_raw = {}
+
+        def load_x(h, g, passes):
+            raw = keep.tile([P, 2, 512 * passes], U8, name="x_raw_%d_%d" % (h, g), tag="x_raw_%d_%d" % (h, g))
+            nc.sync.dma_start(out=raw[:], in_=x_rows[:, 2 * h : 2 * h + 2, 512 * g : 512 * (g + passes)])
+            for i in range(passes):
+                x_raw[h, g + i] = raw[:, :, 512 * i : 512 * i + 512]
+
+        def load_packed_scales(tile, scales):
+            src = scales.bitcast(I32)
+            for quad in range(4):
+                nc.sync.dma_start(out=tile[32 * quad : 32 * quad + 16, :].bitcast(I32), in_=src[:, 4 * quad : 4 * quad + 4, :])
+
+        load_x(0, 0, 1)
+        load_x(0, 1, 1)
+        load_x(0, 2, 2)
+        load_packed_scales(wd_sc, wd_scales)
+        wd = []
+        wd_src = wd_words.rearrange("g p n t -> g p (n t)").bitcast(I32)
+        for g in range(G):
+            w = keep.tile([P, L], U32, name="wd_%d" % g, tag="wd_%d" % g, align_bytes=64)
+            nc.sync.dma_start(out=w[:].bitcast(I32), in_=wd_src[g])
+            wd.append(w)
+        load_x(1, 0, 2)
+        load_x(1, 2, 2)
+        cos_sb = keep.tile([P, MT, D // 2], BF16)
+        sin_sb = keep.tile([P, MT, D // 2], BF16)
+        nc.sync.dma_start(out=cos_sb[:], in_=freqs_cos.rearrange("(m p) j -> p m j", p=P))
+        nc.sync.dma_start(out=sin_sb[:], in_=freqs_sin.rearrange("(m p) j -> p m j", p=P))
+        load_packed_scales(wq_sc, wq_scales)
+        wq = []
+        wq_src = wq_words.rearrange("g p n t -> g p (n t)").bitcast(I32).rearrange("g p n -> p g n")
+
+        def load_wq(n):
+            w = keep.tile([P, G, 512], U32, name="wq_%d" % n, tag="wq_%d" % n, align_bytes=64)
+            for g in range(0, G, 2):
+                nc.sync.dma_start(out=w[:, g : g + 2, :].bitcast(I32), in_=wq_src[:, g : g + 2, 512 * n : 512 * n + 512])
+            wq.append(w)
+
+        load_wq(0)
+        wu = keep.tile([P, 2 * D], U32, align_bytes=64)
+        for i, (words, scales) in enumerate(((wk_words, wk_scales), (wv_words, wv_scales))):
+            cols = slice(D * i, D * i + D)
+            nc.sync.dma_start(out=wu[:, cols].bitcast(I32), in_=words.rearrange("g p n t -> (g p) (n t)").bitcast(I32))
+            src = scales.bitcast(I32)
+            for quad in range(4):
+                nc.sync.dma_start(out=wu_sc[32 * quad : 32 * quad + 4, cols].bitcast(I32), in_=src[0, 4 * quad : 4 * quad + 4, :])
+        for n in range(1, NQ):
+            load_wq(n)
+
+        cs = keep.tile([P, MT, 2, D], F32)
+        nc.gpsimd.tensor_scalar(
+            out=cs[:, :, 0, :].rearrange("p m (j e) -> p m j e", e=2),
+            in0=cos_sb[:].unsqueeze(3).to_broadcast([P, MT, D // 2, 2]),
+            scalar1=1.0, scalar2=0.0, op0=MULT, op1=ADD,
+        )
+        for e, sign in ((0, 1.0), (1, -1.0)):
+            nc.gpsimd.tensor_scalar(
+                out=cs[:, :, 1, e::2], in0=sin_sb[:], scalar1=sign, scalar2=0.0, op0=MULT, op1=ADD,
+            )
+
+        x_codes, x_planes = [], []
+        for h in range(2):
+            codes = keep.tile([P, G, HALF], U32, name="x_codes_%d" % h, tag="x_codes_%d" % h, align_bytes=64)
+            planes = keep.tile([P, G, HALF], U8, name="x_planes_%d" % h, tag="x_planes_%d" % h, align_bytes=64)
+            x_codes.append(codes)
+            x_planes.append(planes)
+        x_bf, x_t, x_grp, kv, lat, q, res = {}, {}, {}, {}, {}, {}, {}
+
+        def cast(i):
+            h, g = divmod(i, G)
+            wide = work.tile([P, 2, 512], BF16, name="wide", tag="wide")
+            for mm in range(2):
+                src = x_raw[h, g][:, mm, :].bitcast(FP8)
+                if i == 0 and mm == 1:
+                    nc.vector.tensor_copy(out=wide[:, mm, :], in_=src)
+                else:
+                    nc.scalar.copy(out=wide[:, mm, :], in_=src)
+            x_bf[i] = wide
+
+        def transpose_x(i):
+            t = bank(i % 4, [P, 2, HALF], "xt")
+            for mm in range(2):
+                words = x_bf[i][:, mm, :].bitcast(F32)
+                for u in range(2):
+                    nc.tensor.transpose(t[:, u, P * mm : P * mm + P], words[:, u:256:2], ident[:])
+            x_t[i] = t
+
+        def scale_x(i):
+            g = i % G
+            grp = work.tile([P, HALF, 4], BF16, name="grp", tag="grp", align_bytes=64)
+            nc.vector.tensor_tensor(
+                out=grp[:].rearrange("p r (u e) -> p r u e", u=2),
+                in0=x_t[i][:].rearrange("p u r -> p (u r)").bitcast(BF16).rearrange("p (u r e) -> p r u e", u=2, e=2),
+                in1=xsc[:, g, :].rearrange("p (u e) -> p u e", u=2).unsqueeze(1).to_broadcast([P, HALF, 2, 2]),
+                op=MULT,
+            )
+            x_grp[i] = grp
+
+        def quantize_x(i):
+            h, g = divmod(i, G)
+            nc.vector.quantize_mx(
+                out=x_codes[h][:, g, :].bitcast(FP8X4), scales=x_planes[h][:, g, :],
+                in_=x_grp[i][:].rearrange("p r t -> p (r t)"),
+            )
+
+        def x_operand(m, g):
+            h, mm = divmod(m, 2)
+            cols = slice(P * mm, P * mm + P)
+            return {"lhsT": x_codes[h][:, g, cols].bitcast(FP8X4), "lhsT_scale": x_planes[h][:, g, cols]}
+
+        def kv_pass(i):
+            h, g = divmod(i, G)
+            for m in (2 * h, 2 * h + 1):
+                if g == 0:
+                    kv[m] = bank(4 + m, [P, L], "kv")
+                nc.tensor.matmul_mx(
+                    out=kv[m][:], rhs=wd[g][:].bitcast(FP8X4), rhs_scale=wd_sc[4 * g :, :],
+                    start=(g == 0), stop=(g == G - 1), **x_operand(m, g),
+                )
+
+        def latent_out(m):
+            t = keep.tile([P, L], BF16, name="lat_%d" % m, tag="lat_%d" % m)
+            nc.scalar.copy(out=t[:], in_=kv[m][:])
+            lat[m] = t
+
+        l_grp = keep.tile([P, T, 4], BF16, align_bytes=64)
+        l_codes = keep.tile([P, T], U32, align_bytes=64)
+        l_planes = keep.tile([P, T], U8, align_bytes=64)
+
+        def latent_transpose(h, b):
+            t = bank(b, [P, 2, HALF], "lt")
+            for mm in range(2):
+                words = lat[2 * h + mm][:].bitcast(F32)
+                for u in range(2):
+                    nc.tensor.transpose(t[:, u, P * mm : P * mm + P], words[:, u:256:2], ident[:])
+            nc.scalar.copy(
+                out=l_grp[:, HALF * h : HALF * h + HALF, :].rearrange("p r t -> p (r t)").bitcast(F32).rearrange("p (r u) -> p r u", u=2),
+                in_=t[:].rearrange("p u r -> p r u"),
+            )
+
+        def latent_quantize():
+            nc.vector.quantize_mx(out=l_codes[:].bitcast(FP8X4), scales=l_planes[:], in_=l_grp[:].rearrange("p r t -> p (r t)"))
+
+        ku = {}
+
+        def kv_up(h, b):
+            t = bank(b, [P, 2, 2 * D], "ku")
+            for mm in range(2):
+                cols = slice(P * (2 * h + mm), P * (2 * h + mm) + P)
+                nc.tensor.matmul_mx(
+                    out=t[:, mm, :], lhsT=l_codes[:, cols].bitcast(FP8X4), lhsT_scale=l_planes[:, cols],
+                    rhs=wu[:].bitcast(FP8X4), rhs_scale=wu_sc[:], start=True, stop=True,
+                )
+            ku[h] = t
+            v_sb = outs.tile([P, 2, D], F32, name="v_sb", tag="v_sb", bufs=2)
+            nc.scalar.copy(out=v_sb[:], in_=t[:, :, D : 2 * D])
+            nc.sync.dma_start(out=v_out.rearrange("b (m p) d -> p (b m) d", p=P)[:, 2 * h : 2 * h + 2, :], in_=v_sb[:])
+
+        def rope_k(h):
+            ab = outs.tile([P, 2, 2, D], F32, name="k_ab", tag="k_ab", bufs=2)
+            nc.vector.tensor_tensor(
+                out=ab[:], in0=ku[h][:, :, 0:D].unsqueeze(1).to_broadcast([P, 2, 2, D]),
+                in1=cs[:, 2 * h : 2 * h + 2, :, :].rearrange("p m c d -> p c m d"), op=MULT,
+            )
+            k_sb = outs.tile([P, 2, D], F32, name="k_sb", tag="k_sb", bufs=2)
+            nc.gpsimd.tensor_tensor(
+                out=k_sb[:].rearrange("p m (j e) -> p (m j) e", e=2),
+                in0=ab[:, 0].rearrange("p m (j e) -> p (m j) e", e=2),
+                in1=ab[:, 1].rearrange("p m (j e) -> p (m j) e", e=2)[:, :, ::-1], op=ADD,
+            )
+            nc.sync.dma_start(out=k_out.rearrange("b (m p) d -> p (b m) d", p=P)[:, 2 * h : 2 * h + 2, :], in_=k_sb[:])
+
+        def query(j, b):
+            n, m = divmod(j, MT)
+            t = bank(b, [P, 512], "q")
+            for g in range(G):
+                nc.tensor.matmul_mx(
+                    out=t[:], rhs=wq[n][:, g, :].bitcast(FP8X4), rhs_scale=wq_sc[4 * g :, 512 * n : 512 * n + 512],
+                    start=(g == 0), stop=(g == G - 1), **x_operand(m, g),
+                )
+            q[j] = t
+
+        q_rows = q_out.rearrange("b t h d -> (b t) (h d)")
+
+        def rope_q(j, pieces=1, adder=nc.gpsimd):
+            n, m = divmod(j, MT)
+            heads = 4 // pieces
+            for i in range(pieces):
+                width = heads * D
+                ab = outs.tile([P, 2, width], F32, name="q_ab", tag="q_ab")
+                nc.vector.tensor_tensor(
+                    out=ab[:].rearrange("p c (h d) -> p c h d", d=D),
+                    in0=q[j][:, width * i : width * i + width].rearrange("p (h d) -> p h d", d=D).unsqueeze(1).to_broadcast([P, 2, heads, D]),
+                    in1=cs[:, m].unsqueeze(2).to_broadcast([P, 2, heads, D]), op=MULT,
+                )
+                q_sb = outs.tile([P, width], F32, name="q_sb", tag="q_sb")
+                adder.tensor_tensor(
+                    out=q_sb[:].rearrange("p (j e) -> p j e", e=2),
+                    in0=ab[:, 0].rearrange("p (j e) -> p j e", e=2),
+                    in1=ab[:, 1].rearrange("p (j e) -> p j e", e=2)[:, :, ::-1], op=ADD,
+                )
+                col = 512 * n + width * i
+                nc.sync.dma_start(out=q_rows[P * m : P * m + P, col : col + width], in_=q_sb[:])
+
+        cast(0); transpose_x(0)
+        cast(1); transpose_x(1); scale_x(0)
+        cast(2); transpose_x(2); scale_x(1); quantize_x(0)
+        cast(3); transpose_x(3); scale_x(2); quantize_x(1)
+        kv_pass(0); kv_pass(1)
+        cast(4); transpose_x(4); cast(5); transpose_x(5)
+        scale_x(3); quantize_x(2); scale_x(4); quantize_x(3)
+        kv_pass(2); kv_pass(3)
+        cast(6); transpose_x(6); cast(7); transpose_x(7)
+        latent_out(0); latent_out(1)
+        scale_x(5); quantize_x(4); scale_x(6); quantize_x(5)
+        kv_pass(4); kv_pass(5)
+        query(0, 0)
+        scale_x(7); quantize_x(6)
+        kv_pass(6)
+        query(1, 1)
+        rope_q(0); quantize_x(7)
+        kv_pass(7)
+        latent_out(2); latent_out(3)
+        query(2, 2); rope_q(1)
+        query(3, 3); rope_q(2)
+        latent_transpose(0, 4); latent_transpose(1, 5)
+        query(4, 6); rope_q(3)
+        latent_quantize()
+        query(5, 7); rope_q(4)
+        kv_up(0, 0); kv_up(1, 1)
+        query(6, 2); rope_q(5); rope_k(0)
+        query(7, 3); rope_q(6); rope_k(1)
+        for j in range(8, 16):
+            query(j, j - 4)
+            rope_q(j - 1)
+        rope_q(15, pieces=2, adder=nc.vector)

@@ -15,277 +15,369 @@ FP8 = mybir.dt.float8_e4m3fn
 FP8X4 = mybir.dt.float8_e4m3fn_x4
 MULT = mybir.AluOpType.mult
 ADD = mybir.AluOpType.add
+COPY = mybir.ActivationFunctionType.Copy
 
 P = 128
-G = C // 512
-MT = T // P
-HALF = 256
-NQ = (HEADS * D) // 512
+K_PASS = 512
+PASSES = C // K_PASS
+TILES = T // P
+HALF = 2 * P
+N_TILE = 512
+HEADS_TILE = N_TILE // D
+PAIR = 2
+
+X_BANKS = (0, 1, 2, 3)
+LATENT_BANKS = (4, 5, 2, 3)
+TURNED_BANKS = (4, 5)
+KEY_VALUE_BANKS = (2, 3)
+FIRST_Q_BANKS, SECOND_Q_BANKS = (6, 7), (0, 1)
+LAST_Q_BANKS = (4, 5, 6, 7)
+IDLE_BANK = 5
 
 
 def tile_attention_pa_w8_kernel(
     tc, x_bytes, x_scale, freqs_cos, freqs_sin,
-    wq_words, wq_scales, wd_words, wd_scales, wk_words, wk_scales, wv_words, wv_scales,
+    wq_words, wq_scales, wkv_down_words, wkv_down_scales, wk_up_words, wk_up_scales, wv_up_words, wv_up_scales,
     q_out, k_out, v_out,
 ):
     nc = tc.nc
     with ExitStack() as ctx:
         keep = ctx.enter_context(tc.tile_pool(name="keep", bufs=1))
-        work = ctx.enter_context(tc.tile_pool(name="work", bufs=3))
-        outs = ctx.enter_context(tc.tile_pool(name="outs", bufs=4))
+        work = ctx.enter_context(tc.tile_pool(name="work", bufs=2))
         psum = ctx.enter_context(tc.psum_pool(name="psum", bufs=1))
         ctx.enter_context(tc.manual_schedule())
 
-        def bank(i, shape, label):
-            t = psum.tile(shape, F32, name="bank%d" % (i % 8), tag="bank%d" % (i % 8))
-            return t
+        def bank(number, shape):
+            tile = psum.tile(shape, F32, name="bank%d" % number, tag="bank%d" % number)
+            return tile
 
         ident = keep.tile([P, P], F32)
         make_identity(nc, ident[:])
-        wd_sc = keep.tile([P, L], U8, align_bytes=64)
-        wq_sc = keep.tile([P, HEADS * D], U8, align_bytes=64)
-        wu_sc = keep.tile([P, 2 * D], U8, align_bytes=64)
-        nc.vector.memset(wd_sc[:].bitcast(I32), 0)
-        nc.vector.memset(wq_sc[:].bitcast(I32), 0)
-        nc.vector.memset(wu_sc[:].bitcast(I32), 0)
+        zeros = keep.tile([P, N_TILE], BF16)
+        nc.vector.memset(zeros[:], 0.0)
+
+        down_planes = keep.tile([P, L], U8, align_bytes=64)
+        q_planes = keep.tile([P, HEADS * D], U8, align_bytes=64)
+        up_planes = keep.tile([P, 2 * D], U8, align_bytes=64)
+        for planes in (down_planes, q_planes, up_planes):
+            nc.vector.memset(planes[:].bitcast(I32), 0)
 
         x_rows = x_bytes.rearrange("b (m p) k -> p (b m) k", p=P)
-        xsc = keep.tile([P, G, 4], F32)
-        nc.scalar.dma_start(out=xsc[:], in_=x_scale.rearrange("a b (g p t) -> p (a b g) t", p=P, t=4))
-        x_raw = {}
+        down_src = wkv_down_words.rearrange("g p n t -> g p (n t)").bitcast(I32)
+        q_src = wq_words.rearrange("g p n t -> g p (n t)").bitcast(I32)
+        x_raw, w_down, w_q = {}, {}, {}
 
-        def load_x(h, g, passes):
-            raw = keep.tile([P, 2, 512 * passes], U8, name="x_raw_%d_%d" % (h, g), tag="x_raw_%d_%d" % (h, g))
-            nc.sync.dma_start(out=raw[:], in_=x_rows[:, 2 * h : 2 * h + 2, 512 * g : 512 * (g + passes)])
-            for i in range(passes):
-                x_raw[h, g + i] = raw[:, :, 512 * i : 512 * i + 512]
+        def load_x(h, g0, g1):
+            raw = keep.tile([P, 2, K_PASS * (g1 - g0)], U8, name="x_raw_%d_%d" % (h, g0), tag="x_raw_%d_%d" % (h, g0))
+            nc.sync.dma_start(out=raw[:], in_=x_rows[:, 2 * h : 2 * h + 2, K_PASS * g0 : K_PASS * g1])
+            for g in range(g0, g1):
+                x_raw[h, g] = raw[:, :, K_PASS * (g - g0) : K_PASS * (g - g0 + 1)]
 
-        def load_packed_scales(tile, scales):
-            src = scales.bitcast(I32)
+        def load_down(g0, g1):
+            words = keep.tile([P, g1 - g0, L], U32, name="w_down_%d" % g0, tag="w_down_%d" % g0, align_bytes=64)
+            nc.sync.dma_start(out=words[:].bitcast(I32), in_=down_src[g0:g1].rearrange("g p n -> p g n"))
+            for g in range(g0, g1):
+                w_down[g] = words[:, g - g0, :]
+
+        def load_q(n, g0, g1):
+            words = keep.tile([P, g1 - g0, N_TILE], U32, name="w_q_%d_%d" % (n, g0), tag="w_q_%d_%d" % (n, g0), align_bytes=64)
+            src = q_src[g0:g1, :, N_TILE * n : N_TILE * (n + 1)]
+            nc.sync.dma_start(out=words[:].bitcast(I32), in_=src.rearrange("g p n -> p g n"))
+            for g in range(g0, g1):
+                w_q[n, g] = words[:, g - g0, :]
+
+        def load_planes(planes, scales):
             for quad in range(4):
-                nc.sync.dma_start(out=tile[32 * quad : 32 * quad + 16, :].bitcast(I32), in_=src[:, 4 * quad : 4 * quad + 4, :])
+                nc.sync.dma_start(
+                    out=planes[32 * quad : 32 * quad + 16, :].bitcast(I32), in_=scales.bitcast(I32)[:, 4 * quad : 4 * quad + 4, :]
+                )
+
+        x_scales = keep.tile([P, PASSES, 4], F32)
+        nc.scalar.dma_start(out=x_scales[:], in_=x_scale.rearrange("a b (g p t) -> p (a b g) t", p=P, t=4))
+        cos_in = keep.tile([P, TILES, D // PAIR], BF16)
+        sin_in = keep.tile([P, TILES, D // PAIR], BF16)
+        nc.gpsimd.dma_start(out=cos_in[:], in_=freqs_cos.rearrange("(m p) j -> p m j", p=P))
+        nc.gpsimd.dma_start(out=sin_in[:], in_=freqs_sin.rearrange("(m p) j -> p m j", p=P))
 
         load_x(0, 0, 1)
-        load_x(0, 1, 1)
-        load_x(0, 2, 2)
-        load_packed_scales(wd_sc, wd_scales)
-        wd = []
-        wd_src = wd_words.rearrange("g p n t -> g p (n t)").bitcast(I32)
-        for g in range(G):
-            w = keep.tile([P, L], U32, name="wd_%d" % g, tag="wd_%d" % g, align_bytes=64)
-            nc.sync.dma_start(out=w[:].bitcast(I32), in_=wd_src[g])
-            wd.append(w)
-        load_x(1, 0, 2)
-        load_x(1, 2, 2)
-        cos_sb = keep.tile([P, MT, D // 2], BF16)
-        sin_sb = keep.tile([P, MT, D // 2], BF16)
-        nc.sync.dma_start(out=cos_sb[:], in_=freqs_cos.rearrange("(m p) j -> p m j", p=P))
-        nc.sync.dma_start(out=sin_sb[:], in_=freqs_sin.rearrange("(m p) j -> p m j", p=P))
-        load_packed_scales(wq_sc, wq_scales)
-        wq = []
-        wq_src = wq_words.rearrange("g p n t -> g p (n t)").bitcast(I32).rearrange("g p n -> p g n")
+        load_x(0, 1, 2)
+        load_x(0, 2, 4)
+        load_x(1, 0, 4)
+        load_planes(q_planes, wq_scales)
+        load_q(0, 0, 1)
+        load_q(0, 1, 2)
+        load_q(0, 2, 4)
+        load_down(0, 2)
+        load_planes(down_planes, wkv_down_scales)
+        load_down(2, 4)
+        for n in range(1, HEADS * D // N_TILE):
+            load_q(n, 0, PASSES)
 
-        def load_wq(n):
-            w = keep.tile([P, G, 512], U32, name="wq_%d" % n, tag="wq_%d" % n, align_bytes=64)
-            for g in range(0, G, 2):
-                nc.sync.dma_start(out=w[:, g : g + 2, :].bitcast(I32), in_=wq_src[:, g : g + 2, 512 * n : 512 * n + 512])
-            wq.append(w)
-
-        load_wq(0)
-        wu = keep.tile([P, 2 * D], U32, align_bytes=64)
-        for i, (words, scales) in enumerate(((wk_words, wk_scales), (wv_words, wv_scales))):
+        w_up = keep.tile([P, 2 * D], U32, align_bytes=64)
+        for i, (words, scales) in enumerate(((wk_up_words, wk_up_scales), (wv_up_words, wv_up_scales))):
             cols = slice(D * i, D * i + D)
-            nc.sync.dma_start(out=wu[:, cols].bitcast(I32), in_=words.rearrange("g p n t -> (g p) (n t)").bitcast(I32))
-            src = scales.bitcast(I32)
+            nc.sync.dma_start(out=w_up[:, cols].bitcast(I32), in_=words.rearrange("g p n t -> (g p) (n t)").bitcast(I32))
             for quad in range(4):
-                nc.sync.dma_start(out=wu_sc[32 * quad : 32 * quad + 4, cols].bitcast(I32), in_=src[0, 4 * quad : 4 * quad + 4, :])
-        for n in range(1, NQ):
-            load_wq(n)
+                nc.sync.dma_start(
+                    out=up_planes[32 * quad : 32 * quad + 4, cols].bitcast(I32), in_=scales.bitcast(I32)[0, 4 * quad : 4 * quad + 4, :]
+                )
 
-        cs = keep.tile([P, MT, 2, D], F32)
-        nc.gpsimd.tensor_scalar(
-            out=cs[:, :, 0, :].rearrange("p m (j e) -> p m j e", e=2),
-            in0=cos_sb[:].unsqueeze(3).to_broadcast([P, MT, D // 2, 2]),
-            scalar1=1.0, scalar2=0.0, op0=MULT, op1=ADD,
-        )
-        for e, sign in ((0, 1.0), (1, -1.0)):
-            nc.gpsimd.tensor_scalar(
-                out=cs[:, :, 1, e::2], in0=sin_sb[:], scalar1=sign, scalar2=0.0, op0=MULT, op1=ADD,
+        angles = keep.tile([P, TILES, 2, D], F32)
+
+        def build_angles():
+            nc.scalar.copy(
+                out=angles[:, :, 0, :].rearrange("p m (j e) -> p m j e", e=PAIR),
+                in_=cos_in[:].unsqueeze(3).to_broadcast([P, TILES, D // PAIR, PAIR]),
             )
+            for e, sign in ((0, -1.0), (1, 1.0)):
+                nc.scalar.activation(out=angles[:, :, 1, e::PAIR], in_=sin_in[:], func=COPY, scale=sign)
 
         x_codes, x_planes = [], []
         for h in range(2):
-            codes = keep.tile([P, G, HALF], U32, name="x_codes_%d" % h, tag="x_codes_%d" % h, align_bytes=64)
-            planes = keep.tile([P, G, HALF], U8, name="x_planes_%d" % h, tag="x_planes_%d" % h, align_bytes=64)
+            codes = keep.tile([P, PASSES, HALF], U32, name="x_codes_%d" % h, tag="x_codes_%d" % h, align_bytes=64)
+            planes = keep.tile([P, PASSES, HALF], U8, name="x_planes_%d" % h, tag="x_planes_%d" % h, align_bytes=64)
             x_codes.append(codes)
             x_planes.append(planes)
-        x_bf, x_t, x_grp, kv, lat, q, res = {}, {}, {}, {}, {}, {}, {}
+        scaled = [keep.tile([P, PASSES, HALF, 4], BF16, name="scaled_%d" % h, tag="scaled_%d" % h, align_bytes=64) for h in range(2)]
+        x_wide = [keep.tile([P, 2, K_PASS], BF16, name="x_wide_%d" % i, tag="x_wide_%d" % i) for i in range(2 * PASSES)]
+        x_turned, x_flat = {}, {}
 
-        def cast(i):
-            h, g = divmod(i, G)
-            wide = work.tile([P, 2, 512], BF16, name="wide", tag="wide")
-            for mm in range(2):
-                src = x_raw[h, g][:, mm, :].bitcast(FP8)
-                if i == 0 and mm == 1:
-                    nc.vector.tensor_copy(out=wide[:, mm, :], in_=src)
-                else:
-                    nc.scalar.copy(out=wide[:, mm, :], in_=src)
-            x_bf[i] = wide
+        def cast(i, mm, copier):
+            h, g = divmod(i, PASSES)
+            copier(out=x_wide[i][:, mm, :], in_=x_raw[h, g][:, mm, :].bitcast(FP8))
 
-        def transpose_x(i):
-            t = bank(i % 4, [P, 2, HALF], "xt")
-            for mm in range(2):
-                words = x_bf[i][:, mm, :].bitcast(F32)
+        def turn(i, tiles):
+            if i not in x_turned:
+                x_turned[i] = bank(X_BANKS[i % 4], [P, 2, HALF])
+            for mm in tiles:
+                words = x_wide[i][:, mm, :].bitcast(F32)
                 for u in range(2):
-                    nc.tensor.transpose(t[:, u, P * mm : P * mm + P], words[:, u:256:2], ident[:])
-            x_t[i] = t
+                    nc.tensor.transpose(x_turned[i][:, u, P * mm : P * mm + P], words[:, u : K_PASS // 2 : 2], ident[:])
 
-        def scale_x(i):
-            g = i % G
-            grp = work.tile([P, HALF, 4], BF16, name="grp", tag="grp", align_bytes=64)
+        def turned_values(i):
+            return x_turned[i][:].rearrange("p u r -> p (u r)").bitcast(BF16).rearrange("p (u r e) -> p u r e", u=2, e=2)
+
+        def scale(i, r0, r1):
+            h, g = divmod(i, PASSES)
+            factors = x_scales[:, g, :].rearrange("p (u e) -> p u e", u=2).unsqueeze(1)
             nc.vector.tensor_tensor(
-                out=grp[:].rearrange("p r (u e) -> p r u e", u=2),
-                in0=x_t[i][:].rearrange("p u r -> p (u r)").bitcast(BF16).rearrange("p (u r e) -> p r u e", u=2, e=2),
-                in1=xsc[:, g, :].rearrange("p (u e) -> p u e", u=2).unsqueeze(1).to_broadcast([P, HALF, 2, 2]),
-                op=MULT,
+                out=scaled[h][:, g, r0:r1, :].rearrange("p r (u e) -> p r u e", u=2),
+                in0=turned_values(i).rearrange("p u r e -> p r u e")[:, r0:r1],
+                in1=factors.to_broadcast([P, r1 - r0, 2, 2]), op=MULT,
             )
-            x_grp[i] = grp
 
-        def quantize_x(i):
-            h, g = divmod(i, G)
-            nc.vector.quantize_mx(
-                out=x_codes[h][:, g, :].bitcast(FP8X4), scales=x_planes[h][:, g, :],
-                in_=x_grp[i][:].rearrange("p r t -> p (r t)"),
+        def scale_on_scalar(i):
+            h, g = divmod(i, PASSES)
+            flat = keep.tile([P, 4, HALF], BF16, name="flat_%d" % i, tag="flat_%d" % i)
+            for t in range(4):
+                nc.scalar.activation(
+                    out=flat[:, t, :], in_=turned_values(i)[:, t // 2, :, t % 2], func=COPY, scale=x_scales[:, g, t : t + 1]
+                )
+            nc.scalar.copy(
+                out=scaled[h][:, g].rearrange("p (c i) t -> p c t i", i=4), in_=flat[:].rearrange("p t (c i) -> p c t i", i=4)
             )
+
+        def quantize(h, g0, g1):
+            nc.vector.quantize_mx(
+                out=x_codes[h][:, g0:g1, :].rearrange("p g r -> p (g r)").bitcast(FP8X4),
+                scales=x_planes[h][:, g0:g1, :].rearrange("p g r -> p (g r)"),
+                in_=scaled[h][:, g0:g1].rearrange("p g r t -> p (g r t)"),
+            )
+
+        latent_sums, q_sums = {}, {}
 
         def x_operand(m, g):
             h, mm = divmod(m, 2)
             cols = slice(P * mm, P * mm + P)
             return {"lhsT": x_codes[h][:, g, cols].bitcast(FP8X4), "lhsT_scale": x_planes[h][:, g, cols]}
 
-        def kv_pass(i):
-            h, g = divmod(i, G)
-            for m in (2 * h, 2 * h + 1):
-                if g == 0:
-                    kv[m] = bank(4 + m, [P, L], "kv")
+        def latent(m):
+            latent_sums[m] = bank(LATENT_BANKS[m], [P, L])
+            for g in range(PASSES):
                 nc.tensor.matmul_mx(
-                    out=kv[m][:], rhs=wd[g][:].bitcast(FP8X4), rhs_scale=wd_sc[4 * g :, :],
-                    start=(g == 0), stop=(g == G - 1), **x_operand(m, g),
+                    out=latent_sums[m][:], rhs=w_down[g].bitcast(FP8X4), rhs_scale=down_planes[4 * g :, :],
+                    start=(g == 0), stop=(g == PASSES - 1), **x_operand(m, g),
                 )
 
-        def latent_out(m):
-            t = keep.tile([P, L], BF16, name="lat_%d" % m, tag="lat_%d" % m)
-            nc.scalar.copy(out=t[:], in_=kv[m][:])
-            lat[m] = t
-
-        l_grp = keep.tile([P, T, 4], BF16, align_bytes=64)
-        l_codes = keep.tile([P, T], U32, align_bytes=64)
-        l_planes = keep.tile([P, T], U8, align_bytes=64)
-
-        def latent_transpose(h, b):
-            t = bank(b, [P, 2, HALF], "lt")
-            for mm in range(2):
-                words = lat[2 * h + mm][:].bitcast(F32)
-                for u in range(2):
-                    nc.tensor.transpose(t[:, u, P * mm : P * mm + P], words[:, u:256:2], ident[:])
-            nc.scalar.copy(
-                out=l_grp[:, HALF * h : HALF * h + HALF, :].rearrange("p r t -> p (r t)").bitcast(F32).rearrange("p (r u) -> p r u", u=2),
-                in_=t[:].rearrange("p u r -> p r u"),
+        def query_pass(n, m, g, number):
+            if g == 0:
+                q_sums[n, m] = bank(number, [P, N_TILE])
+            nc.tensor.matmul_mx(
+                out=q_sums[n, m][:], rhs=w_q[n, g].bitcast(FP8X4), rhs_scale=q_planes[4 * g :, N_TILE * n : N_TILE * (n + 1)],
+                start=(g == 0), stop=(g == PASSES - 1), **x_operand(m, g),
             )
 
-        def latent_quantize():
-            nc.vector.quantize_mx(out=l_codes[:].bitcast(FP8X4), scales=l_planes[:], in_=l_grp[:].rearrange("p r t -> p (r t)"))
+        def query(n, m, number):
+            for g in range(PASSES):
+                query_pass(n, m, g, number)
 
-        ku = {}
+        def first_queries(g):
+            for m in (0, 1):
+                query_pass(0, m, g, FIRST_Q_BANKS[m])
 
-        def kv_up(h, b):
-            t = bank(b, [P, 2, 2 * D], "ku")
+        latent_bf = [keep.tile([P, L], BF16, name="latent_bf_%d" % m, tag="latent_bf_%d" % m) for m in range(TILES)]
+        latent_kt = keep.tile([P, T, 4], BF16, align_bytes=64)
+        latent_codes = keep.tile([P, T], U32, align_bytes=64)
+        latent_planes = keep.tile([P, T], U8, align_bytes=64)
+        key_value = {}
+
+        def round_latent(m):
+            nc.scalar.copy(out=latent_bf[m][:], in_=latent_sums[m][:])
+
+        def turn_latent(h):
+            turned = bank(TURNED_BANKS[h], [P, 2, HALF])
+            for mm in range(2):
+                words = latent_bf[2 * h + mm][:].bitcast(F32)
+                for u in range(2):
+                    nc.tensor.transpose(turned[:, u, P * mm : P * mm + P], words[:, u : L // 2 : 2], ident[:])
+            pairs = latent_kt[:, HALF * h : HALF * h + HALF, :].rearrange("p r t -> p (r t)").bitcast(F32)
+            nc.scalar.copy(out=pairs.rearrange("p (r u) -> p r u", u=2), in_=turned[:].rearrange("p u r -> p r u"))
+
+        def quantize_latent():
+            nc.vector.quantize_mx(
+                out=latent_codes[:].bitcast(FP8X4), scales=latent_planes[:], in_=latent_kt[:].rearrange("p r t -> p (r t)")
+            )
+
+        def keys_and_values(h):
+            sums = key_value[h] = bank(KEY_VALUE_BANKS[h], [P, 2, 2 * D])
             for mm in range(2):
                 cols = slice(P * (2 * h + mm), P * (2 * h + mm) + P)
                 nc.tensor.matmul_mx(
-                    out=t[:, mm, :], lhsT=l_codes[:, cols].bitcast(FP8X4), lhsT_scale=l_planes[:, cols],
-                    rhs=wu[:].bitcast(FP8X4), rhs_scale=wu_sc[:], start=True, stop=True,
+                    out=sums[:, mm, :], lhsT=latent_codes[:, cols].bitcast(FP8X4), lhsT_scale=latent_planes[:, cols],
+                    rhs=w_up[:].bitcast(FP8X4), rhs_scale=up_planes[:], start=True, stop=True,
                 )
-            ku[h] = t
-            v_sb = outs.tile([P, 2, D], F32, name="v_sb", tag="v_sb", bufs=2)
-            nc.scalar.copy(out=v_sb[:], in_=t[:, :, D : 2 * D])
+            v_sb = work.tile([P, 2, D], F32)
+            nc.scalar.copy(out=v_sb[:], in_=sums[:, :, D : 2 * D])
             nc.sync.dma_start(out=v_out.rearrange("b (m p) d -> p (b m) d", p=P)[:, 2 * h : 2 * h + 2, :], in_=v_sb[:])
 
-        def rope_k(h):
-            ab = outs.tile([P, 2, 2, D], F32, name="k_ab", tag="k_ab", bufs=2)
-            nc.vector.tensor_tensor(
-                out=ab[:], in0=ku[h][:, :, 0:D].unsqueeze(1).to_broadcast([P, 2, 2, D]),
-                in1=cs[:, 2 * h : 2 * h + 2, :, :].rearrange("p m c d -> p c m d"), op=MULT,
-            )
-            k_sb = outs.tile([P, 2, D], F32, name="k_sb", tag="k_sb", bufs=2)
-            nc.gpsimd.tensor_tensor(
-                out=k_sb[:].rearrange("p m (j e) -> p (m j) e", e=2),
-                in0=ab[:, 0].rearrange("p m (j e) -> p (m j) e", e=2),
-                in1=ab[:, 1].rearrange("p m (j e) -> p (m j) e", e=2)[:, :, ::-1], op=ADD,
-            )
-            nc.sync.dma_start(out=k_out.rearrange("b (m p) d -> p (b m) d", p=P)[:, 2 * h : 2 * h + 2, :], in_=k_sb[:])
+        def paired(ap):
+            return ap.rearrange("p h (j e) -> p h j e", e=PAIR)
 
-        def query(j, b):
-            n, m = divmod(j, MT)
-            t = bank(b, [P, 512], "q")
-            for g in range(G):
-                nc.tensor.matmul_mx(
-                    out=t[:], rhs=wq[n][:, g, :].bitcast(FP8X4), rhs_scale=wq_sc[4 * g :, 512 * n : 512 * n + 512],
-                    start=(g == 0), stop=(g == G - 1), **x_operand(m, g),
-                )
-            q[j] = t
+        def swapped(ap):
+            return paired(ap)[:, :, :, ::-1]
+
+        k_products = keep.tile([P, 2, TILES, D], F32)
+        k_sb = keep.tile([P, TILES, D], F32)
+
+        def multiply_k(h):
+            ms = slice(2 * h, 2 * h + 2)
+            u = key_value[h][:, :, 0:D]
+            nc.vector.tensor_tensor(out=k_products[:, 0, ms, :], in0=u, in1=angles[:, ms, 0, :], op=MULT)
+            nc.vector.tensor_tensor(out=paired(k_products[:, 1, ms, :]), in0=swapped(u), in1=paired(angles[:, ms, 1, :]), op=MULT)
+
+        def add_k():
+            nc.gpsimd.tensor_tensor(out=k_sb[:], in0=k_products[:, 0], in1=k_products[:, 1], op=ADD)
+            nc.sync.dma_start(out=k_out.rearrange("b (m p) d -> p (b m) d", p=P), in_=k_sb[:])
 
         q_rows = q_out.rearrange("b t h d -> (b t) (h d)")
+        q_products = {}
 
-        def rope_q(j, pieces=1, adder=nc.gpsimd):
-            n, m = divmod(j, MT)
-            heads = 4 // pieces
-            for i in range(pieces):
-                width = heads * D
-                ab = outs.tile([P, 2, width], F32, name="q_ab", tag="q_ab")
-                nc.vector.tensor_tensor(
-                    out=ab[:].rearrange("p c (h d) -> p c h d", d=D),
-                    in0=q[j][:, width * i : width * i + width].rearrange("p (h d) -> p h d", d=D).unsqueeze(1).to_broadcast([P, 2, heads, D]),
-                    in1=cs[:, m].unsqueeze(2).to_broadcast([P, 2, heads, D]), op=MULT,
-                )
-                q_sb = outs.tile([P, width], F32, name="q_sb", tag="q_sb")
-                adder.tensor_tensor(
-                    out=q_sb[:].rearrange("p (j e) -> p j e", e=2),
-                    in0=ab[:, 0].rearrange("p (j e) -> p j e", e=2),
-                    in1=ab[:, 1].rearrange("p (j e) -> p j e", e=2)[:, :, ::-1], op=ADD,
-                )
-                col = 512 * n + width * i
-                nc.sync.dma_start(out=q_rows[P * m : P * m + P, col : col + width], in_=q_sb[:])
+        def multiply_q(n, m, c0=0, c1=N_TILE):
+            heads = (c1 - c0) // D
+            products = q_products[n, m, c0] = work.tile([P, 2, c1 - c0], F32, name="q_products", tag="q_products", bufs=12)
+            by_head = lambda ap: ap.rearrange("p (h d) -> p h d", d=D)
+            spread = lambda ap: ap.unsqueeze(1).to_broadcast([P, heads, D])
+            u = by_head(q_sums[n, m][:, c0:c1])
+            nc.vector.tensor_tensor(out=by_head(products[:, 0]), in0=u, in1=spread(angles[:, m, 0, :]), op=MULT)
+            nc.vector.tensor_tensor(
+                out=paired(by_head(products[:, 1])), in0=swapped(u), in1=paired(spread(angles[:, m, 1, :])), op=MULT
+            )
 
-        cast(0); transpose_x(0)
-        cast(1); transpose_x(1); scale_x(0)
-        cast(2); transpose_x(2); scale_x(1); quantize_x(0)
-        cast(3); transpose_x(3); scale_x(2); quantize_x(1)
-        kv_pass(0); kv_pass(1)
-        cast(4); transpose_x(4); cast(5); transpose_x(5)
-        scale_x(3); quantize_x(2); scale_x(4); quantize_x(3)
-        kv_pass(2); kv_pass(3)
-        cast(6); transpose_x(6); cast(7); transpose_x(7)
-        latent_out(0); latent_out(1)
-        scale_x(5); quantize_x(4); scale_x(6); quantize_x(5)
-        kv_pass(4); kv_pass(5)
-        query(0, 0)
-        scale_x(7); quantize_x(6)
-        kv_pass(6)
-        query(1, 1)
-        rope_q(0); quantize_x(7)
-        kv_pass(7)
-        latent_out(2); latent_out(3)
-        query(2, 2); rope_q(1)
-        query(3, 3); rope_q(2)
-        latent_transpose(0, 4); latent_transpose(1, 5)
-        query(4, 6); rope_q(3)
-        latent_quantize()
-        query(5, 7); rope_q(4)
-        kv_up(0, 0); kv_up(1, 1)
-        query(6, 2); rope_q(5); rope_k(0)
-        query(7, 3); rope_q(6); rope_k(1)
-        for j in range(8, 16):
-            query(j, j - 4)
-            rope_q(j - 1)
-        rope_q(15, pieces=2, adder=nc.vector)
+        def add_q(n, m, c0=0, c1=N_TILE, engine=nc.gpsimd):
+            q_sb = work.tile([P, c1 - c0], F32, name="q_sb", tag="q_sb", bufs=17)
+            products = q_products[n, m, c0]
+            engine.tensor_tensor(out=q_sb[:], in0=products[:, 0], in1=products[:, 1], op=ADD)
+            nc.sync.dma_start(out=q_rows[P * m : P * m + P, N_TILE * n + c0 : N_TILE * n + c1], in_=q_sb[:])
+
+        def rotate_q(n, ms):
+            for m in ms:
+                multiply_q(n, m)
+                add_q(n, m)
+
+        def query_two(n, ms, numbers):
+            for m, number in zip(ms, numbers):
+                query(n, m, number)
+
+        def keep_busy(times):
+            idle = bank(IDLE_BANK, [P, N_TILE])
+            for i in range(times):
+                nc.tensor.matmul(idle[:], lhsT=zeros[:, 0:P], rhs=zeros[:], start=True, stop=True)
+
+        keep_busy(6)
+        for i in (0, 1):
+            for mm in (0, 1):
+                cast(i, mm, nc.vector.tensor_copy)
+                turn(i, (mm,))
+        for i in (2, 3):
+            cast(i, 0, nc.scalar.copy)
+            cast(i, 1, nc.vector.tensor_copy)
+            turn(i, (1, 0))
+            keep_busy(1)
+
+        scale(0, 0, P)
+        scale(0, P, HALF)
+        for i in (1, 2, 3):
+            scale(i, 0, P)
+            quantize(0, i - 1, i)
+            scale(i, P, HALF)
+
+        for i in (4, 5, 6, 7):
+            for mm in (0, 1):
+                cast(i, mm, nc.scalar.copy)
+        build_angles()
+        first_queries(0)
+        first_queries(1)
+        turn(4, (0, 1))
+        turn(5, (0, 1))
+        first_queries(2)
+        turn(6, (0, 1))
+        turn(7, (0, 1))
+        scale(4, 0, HALF)
+        quantize(0, 3, 4)
+        first_queries(3)
+        scale(5, 0, HALF)
+        scale(6, 0, HALF)
+        scale_on_scalar(7)
+
+        latent(0)
+        latent(1)
+        rotate_q(0, (0, 1))
+        query_two(1, (0, 1), SECOND_Q_BANKS)
+        quantize(1, 0, PASSES)
+        rotate_q(1, (0, 1))
+        query_two(2, (0, 1), FIRST_Q_BANKS)
+
+        latent(2)
+        query_two(0, (2, 3), SECOND_Q_BANKS)
+        for m in (0, 1, 2):
+            round_latent(m)
+        rotate_q(2, (0, 1))
+        rotate_q(0, (2, 3))
+        latent(3)
+        round_latent(3)
+        query_two(1, (2, 3), FIRST_Q_BANKS)
+        query(2, 2, SECOND_Q_BANKS[0])
+        turn_latent(0)
+        turn_latent(1)
+        rotate_q(1, (2, 3))
+        rotate_q(2, (2,))
+        query(2, 3, SECOND_Q_BANKS[1])
+        quantize_latent()
+
+        query(3, 0, LAST_Q_BANKS[0])
+        keys_and_values(0)
+        keys_and_values(1)
+        query(3, 1, LAST_Q_BANKS[1])
+        rotate_q(2, (3,))
+        rotate_q(3, (0,))
+        multiply_k(0)
+        multiply_k(1)
+        add_k()
+        query_two(3, (2, 3), LAST_Q_BANKS[2:])
+        rotate_q(3, (1,))
+        multiply_q(3, 2)
+        multiply_q(3, 3, 0, N_TILE // 2)
+        multiply_q(3, 3, N_TILE // 2, N_TILE)
+        add_q(3, 2)
+        add_q(3, 3, 0, N_TILE // 2, nc.vector)
+        add_q(3, 3, N_TILE // 2, N_TILE, nc.vector)

from contextlib import ExitStack

import concourse.mybir as mybir
from concourse.masks import make_identity

T, C, HEADS, D, L = 512, 2048, 16, 128, 512
FLOPS = 2 * T * C * (HEADS * D + L) + 2 * T * L * 2 * D

F32 = mybir.dt.float32
BF16 = mybir.dt.bfloat16
I32 = mybir.dt.int32
U32 = mybir.dt.uint32
U8 = mybir.dt.uint8
FP8 = mybir.dt.float8_e4m3fn
FP8X4 = mybir.dt.float8_e4m3fn_x4
MULT = mybir.AluOpType.mult
ADD = mybir.AluOpType.add
COPY = mybir.ActivationFunctionType.Copy

P = 128
K_PASS = 512
PASSES = C // K_PASS
TILES = T // P
HALF = 2 * P
N_TILE = 512
HEADS_TILE = N_TILE // D
PAIR = 2

X_BANKS = (0, 1, 2, 3)
LATENT_BANKS = (4, 5, 2, 3)
TURNED_BANKS = (4, 5)
KEY_VALUE_BANKS = (2, 3)
FIRST_Q_BANKS, SECOND_Q_BANKS = (6, 7), (0, 1)
LAST_Q_BANKS = (4, 5, 6, 7)
IDLE_BANK = 5


def tile_attention_pa_w8_kernel(
    tc, x_bytes, x_scale, freqs_cos, freqs_sin,
    wq_words, wq_scales, wkv_down_words, wkv_down_scales, wk_up_words, wk_up_scales, wv_up_words, wv_up_scales,
    q_out, k_out, v_out,
):
    nc = tc.nc
    with ExitStack() as ctx:
        keep = ctx.enter_context(tc.tile_pool(name="keep", bufs=1))
        work = ctx.enter_context(tc.tile_pool(name="work", bufs=2))
        psum = ctx.enter_context(tc.psum_pool(name="psum", bufs=1))
        ctx.enter_context(tc.manual_schedule())

        def bank(number, shape):
            tile = psum.tile(shape, F32, name="bank%d" % number, tag="bank%d" % number)
            return tile

        ident = keep.tile([P, P], F32)
        make_identity(nc, ident[:])
        zeros = keep.tile([P, N_TILE], BF16)
        nc.vector.memset(zeros[:], 0.0)

        down_planes = keep.tile([P, L], U8, align_bytes=64)
        q_planes = keep.tile([P, HEADS * D], U8, align_bytes=64)
        up_planes = keep.tile([P, 2 * D], U8, align_bytes=64)
        for planes in (down_planes, q_planes, up_planes):
            nc.vector.memset(planes[:].bitcast(I32), 0)

        x_rows = x_bytes.rearrange("b (m p) k -> p (b m) k", p=P)
        down_src = wkv_down_words.rearrange("g p n t -> g p (n t)").bitcast(I32)
        q_src = wq_words.rearrange("g p n t -> g p (n t)").bitcast(I32)
        x_raw, w_down, w_q = {}, {}, {}

        def load_x(h, g0, g1):
            raw = keep.tile([P, 2, K_PASS * (g1 - g0)], U8, name="x_raw_%d_%d" % (h, g0), tag="x_raw_%d_%d" % (h, g0))
            nc.sync.dma_start(out=raw[:], in_=x_rows[:, 2 * h : 2 * h + 2, K_PASS * g0 : K_PASS * g1])
            for g in range(g0, g1):
                x_raw[h, g] = raw[:, :, K_PASS * (g - g0) : K_PASS * (g - g0 + 1)]

        def load_down(g0, g1):
            words = keep.tile([P, g1 - g0, L], U32, name="w_down_%d" % g0, tag="w_down_%d" % g0, align_bytes=64)
            nc.sync.dma_start(out=words[:].bitcast(I32), in_=down_src[g0:g1].rearrange("g p n -> p g n"))
            for g in range(g0, g1):
                w_down[g] = words[:, g - g0, :]

        def load_q(n, g0, g1):
            words = keep.tile([P, g1 - g0, N_TILE], U32, name="w_q_%d_%d" % (n, g0), tag="w_q_%d_%d" % (n, g0), align_bytes=64)
            src = q_src[g0:g1, :, N_TILE * n : N_TILE * (n + 1)]
            nc.sync.dma_start(out=words[:].bitcast(I32), in_=src.rearrange("g p n -> p g n"))
            for g in range(g0, g1):
                w_q[n, g] = words[:, g - g0, :]

        def load_planes(planes, scales):
            for quad in range(4):
                nc.sync.dma_start(
                    out=planes[32 * quad : 32 * quad + 16, :].bitcast(I32), in_=scales.bitcast(I32)[:, 4 * quad : 4 * quad + 4, :]
                )

        x_scales = keep.tile([P, PASSES, 4], F32)
        nc.scalar.dma_start(out=x_scales[:], in_=x_scale.rearrange("a b (g p t) -> p (a b g) t", p=P, t=4))
        cos_in = keep.tile([P, TILES, D // PAIR], BF16)
        sin_in = keep.tile([P, TILES, D // PAIR], BF16)
        nc.gpsimd.dma_start(out=cos_in[:], in_=freqs_cos.rearrange("(m p) j -> p m j", p=P))
        nc.gpsimd.dma_start(out=sin_in[:], in_=freqs_sin.rearrange("(m p) j -> p m j", p=P))

        load_x(0, 0, 1)
        load_x(0, 1, 2)
        load_x(0, 2, 4)
        load_x(1, 0, 4)
        load_planes(q_planes, wq_scales)
        load_q(0, 0, 1)
        load_q(0, 1, 2)
        load_q(0, 2, 4)
        load_down(0, 2)
        load_planes(down_planes, wkv_down_scales)
        load_down(2, 4)
        for n in range(1, HEADS * D // N_TILE):
            load_q(n, 0, PASSES)

        w_up = keep.tile([P, 2 * D], U32, align_bytes=64)
        for i, (words, scales) in enumerate(((wk_up_words, wk_up_scales), (wv_up_words, wv_up_scales))):
            cols = slice(D * i, D * i + D)
            nc.sync.dma_start(out=w_up[:, cols].bitcast(I32), in_=words.rearrange("g p n t -> (g p) (n t)").bitcast(I32))
            for quad in range(4):
                nc.sync.dma_start(
                    out=up_planes[32 * quad : 32 * quad + 4, cols].bitcast(I32), in_=scales.bitcast(I32)[0, 4 * quad : 4 * quad + 4, :]
                )

        angles = keep.tile([P, TILES, 2, D], F32)

        def build_angles():
            nc.scalar.copy(
                out=angles[:, :, 0, :].rearrange("p m (j e) -> p m j e", e=PAIR),
                in_=cos_in[:].unsqueeze(3).to_broadcast([P, TILES, D // PAIR, PAIR]),
            )
            for e, sign in ((0, -1.0), (1, 1.0)):
                nc.scalar.activation(out=angles[:, :, 1, e::PAIR], in_=sin_in[:], func=COPY, scale=sign)

        x_codes, x_planes = [], []
        for h in range(2):
            codes = keep.tile([P, PASSES, HALF], U32, name="x_codes_%d" % h, tag="x_codes_%d" % h, align_bytes=64)
            planes = keep.tile([P, PASSES, HALF], U8, name="x_planes_%d" % h, tag="x_planes_%d" % h, align_bytes=64)
            x_codes.append(codes)
            x_planes.append(planes)
        scaled = [keep.tile([P, PASSES, HALF, 4], BF16, name="scaled_%d" % h, tag="scaled_%d" % h, align_bytes=64) for h in range(2)]
        x_wide = [keep.tile([P, 2, K_PASS], BF16, name="x_wide_%d" % i, tag="x_wide_%d" % i) for i in range(2 * PASSES)]
        x_turned, x_flat = {}, {}

        def cast(i, mm, copier):
            h, g = divmod(i, PASSES)
            copier(out=x_wide[i][:, mm, :], in_=x_raw[h, g][:, mm, :].bitcast(FP8))

        def turn(i, tiles):
            if i not in x_turned:
                x_turned[i] = bank(X_BANKS[i % 4], [P, 2, HALF])
            for mm in tiles:
                words = x_wide[i][:, mm, :].bitcast(F32)
                for u in range(2):
                    nc.tensor.transpose(x_turned[i][:, u, P * mm : P * mm + P], words[:, u : K_PASS // 2 : 2], ident[:])

        def turned_values(i):
            return x_turned[i][:].rearrange("p u r -> p (u r)").bitcast(BF16).rearrange("p (u r e) -> p u r e", u=2, e=2)

        def scale(i, r0, r1):
            h, g = divmod(i, PASSES)
            factors = x_scales[:, g, :].rearrange("p (u e) -> p u e", u=2).unsqueeze(1)
            nc.vector.tensor_tensor(
                out=scaled[h][:, g, r0:r1, :].rearrange("p r (u e) -> p r u e", u=2),
                in0=turned_values(i).rearrange("p u r e -> p r u e")[:, r0:r1],
                in1=factors.to_broadcast([P, r1 - r0, 2, 2]), op=MULT,
            )

        def scale_on_scalar(i):
            h, g = divmod(i, PASSES)
            flat = keep.tile([P, 4, HALF], BF16, name="flat_%d" % i, tag="flat_%d" % i)
            for t in range(4):
                nc.scalar.activation(
                    out=flat[:, t, :], in_=turned_values(i)[:, t // 2, :, t % 2], func=COPY, scale=x_scales[:, g, t : t + 1]
                )
            nc.scalar.copy(
                out=scaled[h][:, g].rearrange("p (c i) t -> p c t i", i=4), in_=flat[:].rearrange("p t (c i) -> p c t i", i=4)
            )

        def quantize(h, g0, g1):
            nc.vector.quantize_mx(
                out=x_codes[h][:, g0:g1, :].rearrange("p g r -> p (g r)").bitcast(FP8X4),
                scales=x_planes[h][:, g0:g1, :].rearrange("p g r -> p (g r)"),
                in_=scaled[h][:, g0:g1].rearrange("p g r t -> p (g r t)"),
            )

        latent_sums, q_sums = {}, {}

        def x_operand(m, g):
            h, mm = divmod(m, 2)
            cols = slice(P * mm, P * mm + P)
            return {"lhsT": x_codes[h][:, g, cols].bitcast(FP8X4), "lhsT_scale": x_planes[h][:, g, cols]}

        def latent(m):
            latent_sums[m] = bank(LATENT_BANKS[m], [P, L])
            for g in range(PASSES):
                nc.tensor.matmul_mx(
                    out=latent_sums[m][:], rhs=w_down[g].bitcast(FP8X4), rhs_scale=down_planes[4 * g :, :],
                    start=(g == 0), stop=(g == PASSES - 1), **x_operand(m, g),
                )

        def query_pass(n, m, g, number):
            if g == 0:
                q_sums[n, m] = bank(number, [P, N_TILE])
            nc.tensor.matmul_mx(
                out=q_sums[n, m][:], rhs=w_q[n, g].bitcast(FP8X4), rhs_scale=q_planes[4 * g :, N_TILE * n : N_TILE * (n + 1)],
                start=(g == 0), stop=(g == PASSES - 1), **x_operand(m, g),
            )

        def query(n, m, number):
            for g in range(PASSES):
                query_pass(n, m, g, number)

        def first_queries(g):
            for m in (0, 1):
                query_pass(0, m, g, FIRST_Q_BANKS[m])

        latent_bf = [keep.tile([P, L], BF16, name="latent_bf_%d" % m, tag="latent_bf_%d" % m) for m in range(TILES)]
        latent_kt = keep.tile([P, T, 4], BF16, align_bytes=64)
        latent_codes = keep.tile([P, T], U32, align_bytes=64)
        latent_planes = keep.tile([P, T], U8, align_bytes=64)
        key_value = {}

        def round_latent(m):
            nc.scalar.copy(out=latent_bf[m][:], in_=latent_sums[m][:])

        def turn_latent(h):
            turned = bank(TURNED_BANKS[h], [P, 2, HALF])
            for mm in range(2):
                words = latent_bf[2 * h + mm][:].bitcast(F32)
                for u in range(2):
                    nc.tensor.transpose(turned[:, u, P * mm : P * mm + P], words[:, u : L // 2 : 2], ident[:])
            pairs = latent_kt[:, HALF * h : HALF * h + HALF, :].rearrange("p r t -> p (r t)").bitcast(F32)
            nc.scalar.copy(out=pairs.rearrange("p (r u) -> p r u", u=2), in_=turned[:].rearrange("p u r -> p r u"))

        def quantize_latent():
            nc.vector.quantize_mx(
                out=latent_codes[:].bitcast(FP8X4), scales=latent_planes[:], in_=latent_kt[:].rearrange("p r t -> p (r t)")
            )

        def keys_and_values(h):
            sums = key_value[h] = bank(KEY_VALUE_BANKS[h], [P, 2, 2 * D])
            for mm in range(2):
                cols = slice(P * (2 * h + mm), P * (2 * h + mm) + P)
                nc.tensor.matmul_mx(
                    out=sums[:, mm, :], lhsT=latent_codes[:, cols].bitcast(FP8X4), lhsT_scale=latent_planes[:, cols],
                    rhs=w_up[:].bitcast(FP8X4), rhs_scale=up_planes[:], start=True, stop=True,
                )
            v_sb = work.tile([P, 2, D], F32)
            nc.scalar.copy(out=v_sb[:], in_=sums[:, :, D : 2 * D])
            nc.sync.dma_start(out=v_out.rearrange("b (m p) d -> p (b m) d", p=P)[:, 2 * h : 2 * h + 2, :], in_=v_sb[:])

        def paired(ap):
            return ap.rearrange("p h (j e) -> p h j e", e=PAIR)

        def swapped(ap):
            return paired(ap)[:, :, :, ::-1]

        k_products = keep.tile([P, 2, TILES, D], F32)
        k_sb = keep.tile([P, TILES, D], F32)

        def multiply_k(h):
            ms = slice(2 * h, 2 * h + 2)
            u = key_value[h][:, :, 0:D]
            nc.vector.tensor_tensor(out=k_products[:, 0, ms, :], in0=u, in1=angles[:, ms, 0, :], op=MULT)
            nc.vector.tensor_tensor(out=paired(k_products[:, 1, ms, :]), in0=swapped(u), in1=paired(angles[:, ms, 1, :]), op=MULT)

        def add_k():
            nc.gpsimd.tensor_tensor(out=k_sb[:], in0=k_products[:, 0], in1=k_products[:, 1], op=ADD)
            nc.sync.dma_start(out=k_out.rearrange("b (m p) d -> p (b m) d", p=P), in_=k_sb[:])

        q_rows = q_out.rearrange("b t h d -> (b t) (h d)")
        q_products = {}

        def multiply_q(n, m, c0=0, c1=N_TILE):
            heads = (c1 - c0) // D
            products = q_products[n, m, c0] = work.tile([P, 2, c1 - c0], F32, name="q_products", tag="q_products", bufs=12)
            by_head = lambda ap: ap.rearrange("p (h d) -> p h d", d=D)
            spread = lambda ap: ap.unsqueeze(1).to_broadcast([P, heads, D])
            u = by_head(q_sums[n, m][:, c0:c1])
            nc.vector.tensor_tensor(out=by_head(products[:, 0]), in0=u, in1=spread(angles[:, m, 0, :]), op=MULT)
            nc.vector.tensor_tensor(
                out=paired(by_head(products[:, 1])), in0=swapped(u), in1=paired(spread(angles[:, m, 1, :])), op=MULT
            )

        def add_q(n, m, c0=0, c1=N_TILE, engine=nc.gpsimd):
            q_sb = work.tile([P, c1 - c0], F32, name="q_sb", tag="q_sb", bufs=17)
            products = q_products[n, m, c0]
            engine.tensor_tensor(out=q_sb[:], in0=products[:, 0], in1=products[:, 1], op=ADD)
            nc.sync.dma_start(out=q_rows[P * m : P * m + P, N_TILE * n + c0 : N_TILE * n + c1], in_=q_sb[:])

        def rotate_q(n, ms):
            for m in ms:
                multiply_q(n, m)
                add_q(n, m)

        def query_two(n, ms, numbers):
            for m, number in zip(ms, numbers):
                query(n, m, number)

        def keep_busy(times):
            idle = bank(IDLE_BANK, [P, N_TILE])
            for i in range(times):
                nc.tensor.matmul(idle[:], lhsT=zeros[:, 0:P], rhs=zeros[:], start=True, stop=True)

        keep_busy(6)
        for i in (0, 1):
            for mm in (0, 1):
                cast(i, mm, nc.vector.tensor_copy)
                turn(i, (mm,))
        for i in (2, 3):
            cast(i, 0, nc.scalar.copy)
            cast(i, 1, nc.vector.tensor_copy)
            turn(i, (1, 0))
            keep_busy(1)

        scale(0, 0, P)
        scale(0, P, HALF)
        for i in (1, 2, 3):
            scale(i, 0, P)
            quantize(0, i - 1, i)
            scale(i, P, HALF)

        for i in (4, 5, 6, 7):
            for mm in (0, 1):
                cast(i, mm, nc.scalar.copy)
        build_angles()
        first_queries(0)
        first_queries(1)
        turn(4, (0, 1))
        turn(5, (0, 1))
        first_queries(2)
        turn(6, (0, 1))
        turn(7, (0, 1))
        scale(4, 0, HALF)
        quantize(0, 3, 4)
        first_queries(3)
        scale(5, 0, HALF)
        scale(6, 0, HALF)
        scale_on_scalar(7)

        latent(0)
        latent(1)
        rotate_q(0, (0, 1))
        query_two(1, (0, 1), SECOND_Q_BANKS)
        quantize(1, 0, PASSES)
        rotate_q(1, (0, 1))
        query_two(2, (0, 1), FIRST_Q_BANKS)

        latent(2)
        query_two(0, (2, 3), SECOND_Q_BANKS)
        for m in (0, 1, 2):
            round_latent(m)
        rotate_q(2, (0, 1))
        rotate_q(0, (2, 3))
        latent(3)
        round_latent(3)
        query_two(1, (2, 3), FIRST_Q_BANKS)
        query(2, 2, SECOND_Q_BANKS[0])
        turn_latent(0)
        turn_latent(1)
        rotate_q(1, (2, 3))
        rotate_q(2, (2,))
        query(2, 3, SECOND_Q_BANKS[1])
        quantize_latent()

        query(3, 0, LAST_Q_BANKS[0])
        keys_and_values(0)
        keys_and_values(1)
        query(3, 1, LAST_Q_BANKS[1])
        rotate_q(2, (3,))
        rotate_q(3, (0,))
        multiply_k(0)
        multiply_k(1)
        add_k()
        query_two(3, (2, 3), LAST_Q_BANKS[2:])
        rotate_q(3, (1,))
        multiply_q(3, 2)
        multiply_q(3, 3, 0, N_TILE // 2)
        multiply_q(3, 3, N_TILE // 2, N_TILE)
        add_q(3, 2)
        add_q(3, 3, 0, N_TILE // 2, nc.vector)
        add_q(3, 3, N_TILE // 2, N_TILE, nc.vector)
